import numpy as np
import ml_dtypes


BF16 = ml_dtypes.bfloat16


def bf(x):
    return np.asarray(x, np.float32).astype(BF16)


def f64(x):
    return np.asarray(x).astype(np.float64)


E2M1 = np.array([0.0, 0.5, 1.0, 1.5, 2.0, 3.0, 4.0, 6.0, -0.0, -0.5, -1.0, -1.5, -2.0, -3.0, -4.0, -6.0])


def pack_weight(w, fmt):
    k, n = w.shape
    w = f64(bf(w)).reshape(k // 32, 32, n)
    amax = np.abs(w).max(1)
    if fmt == "e4m3":
        byte = np.frexp(amax)[1] - 1 + 127 - 7
    else:
        mant, ex = np.frexp(amax / 6.0)
        byte = np.where(mant > 0.5, ex, ex - 1) + 127
    byte = np.clip(np.where(amax > 0, byte, 1), 1, 254)
    scaled = (w * np.exp2(127.0 - byte)[:, None, :]).reshape(k, n).astype(np.float32)
    by_word = np.ascontiguousarray(scaled.reshape(k // 512, 128, 4, n).transpose(0, 1, 3, 2))
    if fmt == "e4m3":
        words = by_word.astype(ml_dtypes.float8_e4m3fn).view(np.uint8)
    else:
        c = by_word.astype(ml_dtypes.float4_e2m1fn).view(np.uint8) & 0xF
        words = c[..., 0::2] | (c[..., 1::2] << 4)
    return np.ascontiguousarray(words), np.ascontiguousarray(byte.astype(np.uint8).reshape(k // 512, 16, n))


def unpack_weight(words, scales, fmt):
    g, p, n, _ = words.shape
    if fmt == "e4m3":
        vals = np.ascontiguousarray(words).view(ml_dtypes.float8_e4m3fn).astype(np.float64)
    else:
        nib = np.empty((g, p, n, 4), np.uint8)
        nib[..., 0::2] = words & 0xF
        nib[..., 1::2] = words >> 4
        vals = E2M1[nib]
    vals = vals * np.repeat(np.exp2(scales.astype(np.float64) - 127.0), 8, axis=1)[..., None]
    return vals.transpose(0, 1, 3, 2).reshape(g * 512, n)

def pack4(w):
    words, scales = pack_weight(w, "e2m1")
    return words.reshape(words.shape[0], 128, -1), scales


def unpack4(words, scales):
    return unpack_weight(words.reshape(words.shape[0], 128, -1, 2), scales, "e2m1")


def kspread(k):
    return np.exp2(np.repeat(np.random.randint(-6, 7, k // 32), 32).astype(np.float64))


B, S, H, N_HEADS, N_KV, D, QB, ORIG_MAX_POS = 1, 2048, 4096, 16, 4, 128, 512, 8192
ROPE_BASE = 5.0e5
ROPE_FACTOR = 8.0
LOW_FREQ, HIGH_FREQ = 1.0, 4.0


def llama3_cos_sin():
    inv_freq = 1.0 / (ROPE_BASE ** (np.arange(0, D, 2) / D))
    wavelen = 2.0 * np.pi / inv_freq
    smooth = np.clip((ORIG_MAX_POS / wavelen - LOW_FREQ) / (HIGH_FREQ - LOW_FREQ), 0.0, 1.0)
    new_inv_freq = (1.0 - smooth) * (inv_freq / ROPE_FACTOR) + smooth * inv_freq
    freqs = np.arange(S)[:, None] * new_inv_freq[None, :]
    emb = np.concatenate([freqs, freqs], axis=-1)
    return np.cos(emb), np.sin(emb)


def rotate_half(x):
    x1, x2 = x[..., : D // 2], x[..., D // 2:]
    return np.concatenate([-x2, x1], axis=-1)


def apply_rope(x, cos, sin):
    return x * cos[None, None, :, :] + rotate_half(x) * sin[None, None, :, :]


def setup_inputs():
    s = kspread(H)
    hidden_states = np.random.standard_normal((B, S, H)) * s
    wq = np.random.standard_normal((N_HEADS * D, H)) / np.sqrt(H) / s[None, :]
    wk = np.random.standard_normal((N_KV * D, H)) / np.sqrt(H) / s[None, :]
    hidden_states_words, hidden_states_scales = pack4(np.ascontiguousarray(hidden_states.reshape(B * S, H).T))
    wq_words, wq_scales = pack4(np.ascontiguousarray(wq.T))
    wk_words, wk_scales = pack4(np.ascontiguousarray(wk.T))
    return {"hidden_states_words": hidden_states_words, "hidden_states_scales": hidden_states_scales,
            "wq_words": wq_words, "wq_scales": wq_scales,
            "wk_words": wk_words, "wk_scales": wk_scales}


def reference(hidden_states_words, hidden_states_scales, wq_words, wq_scales, wk_words, wk_scales):
    xq = unpack4(hidden_states_words, hidden_states_scales).T.reshape(B, S, H)
    q = (xq @ unpack4(wq_words, wq_scales)).reshape(B, S, N_HEADS, D).transpose(0, 2, 1, 3)
    k = (xq @ unpack4(wk_words, wk_scales)).reshape(B, S, N_KV, D).transpose(0, 2, 1, 3)
    cos, sin = llama3_cos_sin()
    return apply_rope(q, cos, sin), apply_rope(k, cos, sin)

@@ -1,0 +1,208 @@
+from contextlib import ExitStack
+
+import concourse.mybir as mybir
+
+F32 = mybir.dt.float32
+I32 = mybir.dt.int32
+U8 = mybir.dt.uint8
+FP4X4 = mybir.dt.float4_e2m1fn_x4
+ALU = mybir.AluOpType
+ACT = mybir.ActivationFunctionType
+
+P = 128
+PASSES = 8
+TOKEN_TILES = 16
+HALF = 64
+TWO_PI = 6.283185307179586
+GRID = 2.0 ** -14
+
+FLOPS = 2 * 2048 * 4096 * 2560
+
+RUNS = ((0, 1), (1, 3), (3, 8))
+
+
+def turns_per_position():
+    g = []
+    for j in range(HALF):
+        inv = 1.0 / (500000.0 ** (2.0 * j / 128.0))
+        wavelen = TWO_PI / inv
+        smooth = min(max((8192.0 / wavelen - 1.0) / 3.0, 0.0), 1.0)
+        g.append(((1.0 - smooth) * (inv / 8.0) + smooth * inv) / TWO_PI)
+    return g
+
+
+def tile_stickyllamaattention_pa_kernel(tc, xw, xs, wqw, wqs, wkw, wks, out_0, out_1):
+    nc = tc.nc
+    g_all = turns_per_position()
+    g_hi = [int(g / GRID) * GRID for g in g_all]
+    g_lo = [g - h for g, h in zip(g_all, g_hi)]
+    n_hi = len([h for h in g_hi if h > 0.0])
+
+    with ExitStack() as ctx:
+        keep = ctx.enter_context(tc.tile_pool(name="keep", bufs=1))
+        work = ctx.enter_context(tc.tile_pool(name="work", bufs=6))
+        psum = ctx.enter_context(tc.psum_pool(name="acc", bufs=8))
+        ctx.enter_context(tc.manual_schedule())
+
+        def load_codes(tile_ap, src):
+            nc.sync.dma_start(out=tile_ap.bitcast(I32), in_=src.bitcast(I32))
+
+        def load_scales(plane, src):
+            for q in range(4):
+                nc.sync.dma_start(
+                    out=plane[32 * q : 32 * q + 4, :, :].bitcast(I32),
+                    in_=src[:, 4 * q : 4 * q + 4, :].rearrange("g r n -> r g n").bitcast(I32),
+                )
+
+        xc_a = [keep.tile([P, 2048], U8, name="xc_a%d" % g, align_bytes=64) for g in range(PASSES)]
+        wc_0 = [keep.tile([P, 1024], U8, name="wc_0%d" % g, align_bytes=64) for g in range(PASSES)]
+        xs_a = [keep.tile([P, b - a, 1024], U8, name="xs_a%d" % a, align_bytes=64) for a, b in RUNS]
+        ws_0 = [keep.tile([P, b - a, 512], U8, name="ws_0%d" % a, align_bytes=64) for a, b in RUNS]
+        xc_b = [keep.tile([P, PASSES, 1024], U8, name="xc_b%d" % c, align_bytes=64) for c in range(2)]
+        xs_b = [keep.tile([P, PASSES, 512], U8, name="xs_b%d" % c, align_bytes=64) for c in range(2)]
+        wc_r = [keep.tile([P, PASSES, 1024], U8, name="wc_r%d" % b, align_bytes=64) for b in range(4)]
+        ws_r = keep.tile([P, PASSES, 1536], U8, name="ws_r", align_bytes=64)
+        ws_k = keep.tile([P, PASSES, 512], U8, name="ws_k", align_bytes=64)
+
+        load_codes(xc_a[0][:], xw[0, :, 0:2048])
+        load_codes(wc_0[0][:], wqw[0, :, 0:1024])
+        for r, (a, b) in enumerate(RUNS):
+            nc.vector.memset(xs_a[r][:].bitcast(I32), 0)
+            nc.vector.memset(ws_0[r][:].bitcast(I32), 0)
+        for r, (a, b) in enumerate(RUNS):
+            load_scales(xs_a[r], xs[a:b, :, 0:1024])
+            load_scales(ws_0[r], wqs[a:b, :, 0:512])
+            for g in range(max(a, 1), b):
+                load_codes(xc_a[g][:], xw[g, :, 0:2048])
+                load_codes(wc_0[g][:], wqw[g, :, 0:1024])
+
+        pos_i = keep.tile([P, TOKEN_TILES], I32, name="pos_i")
+        nc.gpsimd.iota(out=pos_i[:], pattern=[[P, TOKEN_TILES]], base=0, channel_multiplier=1)
+        for c in range(2):
+            nc.gpsimd.memset(xs_b[c][:].bitcast(F32), 0.0)
+        nc.gpsimd.memset(ws_r[:].bitcast(F32), 0.0)
+        nc.gpsimd.memset(ws_k[:].bitcast(F32), 0.0)
+
+        for c in range(2):
+            load_scales(xs_b[c], xs[:, :, 1024 + 512 * c : 1536 + 512 * c])
+            load_codes(xc_b[c][:], xw[:, :, 2048 + 1024 * c : 3072 + 1024 * c].rearrange("g p n -> p g n"))
+        load_scales(ws_r, wqs[:, :, 512:2048])
+        load_scales(ws_k, wks[:, :, :])
+        for b in range(3):
+            load_codes(wc_r[b][:], wqw[:, :, 1024 * (b + 1) : 1024 * (b + 2)].rearrange("g p n -> p g n"))
+        load_codes(wc_r[3][:], wkw[:, :, :].rearrange("g p n -> p g n"))
+
+        warm = keep.tile([P, 1], F32, name="warm")
+        nc.vector.memset(warm[:], 0.0)
+        nc.scalar.activation(out=warm[:], in_=warm[:], func=ACT.Sin)
+
+        pos_f = keep.tile([P, TOKEN_TILES], F32, name="pos_f")
+        nc.vector.tensor_copy(out=pos_f[:], in_=pos_i[:])
+
+        rr = keep.tile([P, TOKEN_TILES, HALF], F32, name="rr")
+        big = keep.tile([P, TOKEN_TILES, n_hi], F32, name="big")
+        whole_i = keep.tile([P, TOKEN_TILES, n_hi], I32, name="whole_i")
+        whole_f = keep.tile([P, TOKEN_TILES, n_hi], F32, name="whole_f")
+        neg_s = keep.tile([P, TOKEN_TILES, HALF], F32, name="neg_s")
+        rc = keep.tile([P, TOKEN_TILES, HALF], F32, name="rc")
+        neg_c = keep.tile([P, TOKEN_TILES, HALF], F32, name="neg_c")
+        cos_t = keep.tile([P, TOKEN_TILES, HALF], F32, name="cos_t")
+        sin_t = keep.tile([P, TOKEN_TILES, HALF], F32, name="sin_t")
+        nsin_t = keep.tile([P, TOKEN_TILES, HALF], F32, name="nsin_t")
+
+        for j in range(n_hi):
+            nc.scalar.activation(out=big[:, :, j], in_=pos_f[:], func=ACT.Copy, scale=g_hi[j])
+        for j in range(HALF):
+            nc.vector.tensor_scalar(out=rr[:, :, j], in0=pos_f[:], scalar1=g_lo[j], scalar2=None, op0=ALU.mult)
+        nc.vector.tensor_copy(out=whole_i[:], in_=big[:])
+        nc.vector.tensor_copy(out=whole_f[:], in_=whole_i[:])
+        nc.vector.tensor_tensor(out=big[:], in0=big[:], in1=whole_f[:], op=ALU.subtract)
+        nc.vector.tensor_tensor(out=rr[:, :, 0:n_hi], in0=rr[:, :, 0:n_hi], in1=big[:], op=ALU.add)
+        flat = "p i j -> p (i j)"
+        nc.vector.scalar_tensor_tensor(
+            out=neg_s[:].rearrange(flat), in0=rr[:].rearrange(flat), scalar=0.5, in1=rr[:].rearrange(flat),
+            op0=ALU.is_gt, op1=ALU.subtract,
+        )
+        nc.vector.tensor_scalar(
+            out=rc[:].rearrange(flat), in0=neg_s[:].rearrange(flat), scalar1=-1.0, scalar2=0.25,
+            op0=ALU.mult, op1=ALU.add,
+        )
+        nc.scalar.activation(out=sin_t[:].rearrange(flat), in_=neg_s[:].rearrange(flat), func=ACT.Sin, scale=-TWO_PI)
+        nc.scalar.activation(out=nsin_t[:].rearrange(flat), in_=neg_s[:].rearrange(flat), func=ACT.Sin, scale=TWO_PI)
+        nc.vector.scalar_tensor_tensor(
+            out=neg_c[:].rearrange(flat), in0=rc[:].rearrange(flat), scalar=0.5, in1=rc[:].rearrange(flat),
+            op0=ALU.is_gt, op1=ALU.subtract,
+        )
+        nc.scalar.activation(out=cos_t[:].rearrange(flat), in_=neg_c[:].rearrange(flat), func=ACT.Sin, scale=-TWO_PI)
+
+        def run_of(g):
+            return [r for r, (a, b) in enumerate(RUNS) if a <= g < b][0]
+
+        def x_ops(i, g):
+            if i < 8:
+                r = run_of(g)
+                return (xc_a[g][:, 256 * i : 256 * (i + 1)], xs_a[r][:, g - RUNS[r][0], 128 * i : 128 * (i + 1)])
+            c, ii = divmod(i - 8, 4)
+            return (xc_b[c][:, g, 256 * ii : 256 * (ii + 1)], xs_b[c][:, g, 128 * ii : 128 * (ii + 1)])
+
+        def w_ops(b, g):
+            if b == 0:
+                r = run_of(g)
+                return (wc_0[g][:, :], ws_0[r][:, g - RUNS[r][0], :])
+            if b < 4:
+                return (wc_r[b - 1][:, g, :], ws_r[:, g, 512 * (b - 1) : 512 * b])
+            return (wc_r[3][:, g, :], ws_k[:, g, :])
+
+        def one_pass(acc, i, b, g, h0=0, nh=4):
+            xcod, xsc = x_ops(i, g)
+            wcod, wsc = w_ops(b, g)
+            nc.tensor.matmul_mx(
+                out=acc[:], lhsT=xcod.bitcast(FP4X4), lhsT_scale=xsc,
+                rhs=wcod[:, 256 * h0 : 256 * (h0 + nh)].bitcast(FP4X4), rhs_scale=wsc[:, P * h0 : P * (h0 + nh)],
+                start=(g == 0), stop=(g == PASSES - 1),
+            )
+
+        def rope_and_store(acc, i, b, adder, queue, h0=0, nh=4):
+            res = work.tile([P, P * nh], F32, name="res", bufs=16)
+            rot = work.tile([P, P * nh], F32, name="rot")
+            nc.vector.tensor_tensor(
+                out=res[:].rearrange("p (u j) -> p u j", j=HALF), in0=acc[:].rearrange("p (u j) -> p u j", j=HALF),
+                in1=cos_t[:, i, :].unsqueeze(1).to_broadcast([P, 2 * nh, HALF]), op=ALU.mult,
+            )
+            a4 = acc[:].rearrange("p (h t j) -> p h t j", t=2, j=HALF)
+            r4 = rot[:].rearrange("p (h t j) -> p h t j", t=2, j=HALF)
+            nc.vector.tensor_tensor(
+                out=r4[:, :, 0, :], in0=a4[:, :, 1, :],
+                in1=nsin_t[:, i, :].unsqueeze(1).to_broadcast([P, nh, HALF]), op=ALU.mult,
+            )
+            nc.vector.tensor_tensor(
+                out=r4[:, :, 1, :], in0=a4[:, :, 0, :],
+                in1=sin_t[:, i, :].unsqueeze(1).to_broadcast([P, nh, HALF]), op=ALU.mult,
+            )
+            adder.tensor_tensor(out=res[:], in0=res[:], in1=rot[:], op=ALU.add)
+            dst = out_0[0, 4 * b + h0 : 4 * b + h0 + nh, :, :] if b < 4 else out_1[0, h0 : h0 + nh, :, :]
+            queue.dma_start(
+                out=dst[:, P * i : P * (i + 1), :].rearrange("h p d -> p h d"),
+                in_=res[:].rearrange("p (h d) -> p h d", h=nh),
+            )
+
+        queues = (nc.scalar, nc.sync)
+
+        first = [psum.tile([P, 512], F32, name="acc") for i in range(8)]
+        for g in range(PASSES):
+            for i in range(8):
+                one_pass(first[i], i, 0, g)
+        for i in range(8):
+            rope_and_store(first[i], i, 0, nc.gpsimd, queues[i % 2])
+
+        for b, i in [(b, i) for b in range(5) for i in range(TOKEN_TILES)][8:-1]:
+            acc = psum.tile([P, 512], F32, name="acc")
+            for g in range(PASSES):
+                one_pass(acc, i, b, g)
+            rope_and_store(acc, i, b, nc.gpsimd, queues[i % 2])
+
+        for n, (h0, nh) in enumerate(((0, 2), (2, 1), (3, 1))):
+            acc = psum.tile([P, P * nh], F32, name="acc")
+            for g in range(PASSES):
+                one_pass(acc, TOKEN_TILES - 1, 4, g, h0, nh)
+            rope_and_store(acc, TOKEN_TILES - 1, 4, nc.gpsimd if n == 0 else nc.vector, queues[(n + 1) % 2], h0, nh)

@@ -61,18 +61,29 @@ def tile_stickyllamaattention_pa_kernel(tc, xw, xs, wqw, wqs, wkw, wks, out_0, o
         xc_b = [keep.tile([P, PASSES, 1024], U8, name="xc_b%d" % c, align_bytes=64) for c in range(2)]
         xs_b = [keep.tile([P, PASSES, 512], U8, name="xs_b%d" % c, align_bytes=64) for c in range(2)]
         wc_r = [keep.tile([P, PASSES, 1024], U8, name="wc_r%d" % b, align_bytes=64) for b in range(4)]
-        ws_r = keep.tile([P, PASSES, 1536], U8, name="ws_r", align_bytes=64)
-        ws_k = keep.tile([P, PASSES, 512], U8, name="ws_k", align_bytes=64)
+        ws_r = [keep.tile([P, PASSES, 512], U8, name="ws_r%d" % b, align_bytes=64) for b in range(4)]
 
+        def load_quadrant(plane, src, q):
+            nc.sync.dma_start(
+                out=plane[32 * q : 32 * q + 32, 0, :].bitcast(I32),
+                in_=src.rearrange("g r n -> (g r) n")[4 * q : 4 * q + 32, :].bitcast(I32),
+            )
+
+        load_quadrant(ws_0[0], wqs[:, :, 0:512], 0)
+        load_quadrant(ws_0[0], wqs[:, :, 0:512], 1)
         load_codes(xc_a[0][:], xw[0, :, 0:2048])
         load_codes(wc_0[0][:], wqw[0, :, 0:1024])
-        for r, (a, b) in enumerate(RUNS):
+        load_quadrant(ws_0[0], wqs[:, :, 0:512], 2)
+        load_quadrant(ws_0[0], wqs[:, :, 0:512], 3)
+        for q in range(4):
+            load_quadrant(xs_a[0], xs[:, :, 0:1024], q)
+        for r in (1, 2):
             nc.vector.memset(xs_a[r][:].bitcast(I32), 0)
             nc.vector.memset(ws_0[r][:].bitcast(I32), 0)
-        for r, (a, b) in enumerate(RUNS):
+        for r, (a, b) in ((1, RUNS[1]), (2, RUNS[2])):
             load_scales(xs_a[r], xs[a:b, :, 0:1024])
             load_scales(ws_0[r], wqs[a:b, :, 0:512])
-            for g in range(max(a, 1), b):
+            for g in range(a, b):
                 load_codes(xc_a[g][:], xw[g, :, 0:2048])
                 load_codes(wc_0[g][:], wqw[g, :, 0:1024])
 
@@ -80,16 +91,16 @@ def tile_stickyllamaattention_pa_kernel(tc, xw, xs, wqw, wqs, wkw, wks, out_0, o
         nc.gpsimd.iota(out=pos_i[:], pattern=[[P, TOKEN_TILES]], base=0, channel_multiplier=1)
         for c in range(2):
             nc.gpsimd.memset(xs_b[c][:].bitcast(F32), 0.0)
-        nc.gpsimd.memset(ws_r[:].bitcast(F32), 0.0)
-        nc.gpsimd.memset(ws_k[:].bitcast(F32), 0.0)
+        for b in range(4):
+            nc.gpsimd.memset(ws_r[b][:].bitcast(F32), 0.0)
 
         for c in range(2):
             load_scales(xs_b[c], xs[:, :, 1024 + 512 * c : 1536 + 512 * c])
             load_codes(xc_b[c][:], xw[:, :, 2048 + 1024 * c : 3072 + 1024 * c].rearrange("g p n -> p g n"))
-        load_scales(ws_r, wqs[:, :, 512:2048])
-        load_scales(ws_k, wks[:, :, :])
         for b in range(3):
+            load_scales(ws_r[b], wqs[:, :, 512 * (b + 1) : 512 * (b + 2)])
             load_codes(wc_r[b][:], wqw[:, :, 1024 * (b + 1) : 1024 * (b + 2)].rearrange("g p n -> p g n"))
+        load_scales(ws_r[3], wks[:, :, :])
         load_codes(wc_r[3][:], wkw[:, :, :].rearrange("g p n -> p g n"))
 
         warm = keep.tile([P, 1], F32, name="warm")
@@ -149,9 +160,7 @@ def tile_stickyllamaattention_pa_kernel(tc, xw, xs, wqw, wqs, wkw, wks, out_0, o
             if b == 0:
                 r = run_of(g)
                 return (wc_0[g][:, :], ws_0[r][:, g - RUNS[r][0], :])
-            if b < 4:
-                return (wc_r[b - 1][:, g, :], ws_r[:, g, 512 * (b - 1) : 512 * b])
-            return (wc_r[3][:, g, :], ws_k[:, g, :])
+            return (wc_r[b - 1][:, g, :], ws_r[b - 1][:, g, :])
 
         def one_pass(acc, i, b, g, h0=0, nh=4):
             xcod, xsc = x_ops(i, g)
@@ -201,8 +210,8 @@ def tile_stickyllamaattention_pa_kernel(tc, xw, xs, wqw, wqs, wkw, wks, out_0, o
                 one_pass(acc, i, b, g)
             rope_and_store(acc, i, b, nc.gpsimd, queues[i % 2])
 
-        for n, (h0, nh) in enumerate(((0, 2), (2, 1), (3, 1))):
+        for n, (h0, nh) in enumerate(((0, 2), (2, 2))):
             acc = psum.tile([P, P * nh], F32, name="acc")
             for g in range(PASSES):
                 one_pass(acc, TOKEN_TILES - 1, 4, g, h0, nh)
-            rope_and_store(acc, TOKEN_TILES - 1, 4, nc.gpsimd if n == 0 else nc.vector, queues[(n + 1) % 2], h0, nh)
+            rope_and_store(acc, TOKEN_TILES - 1, 4, nc.vector, queues[(n + 1) % 2], h0, nh)

@@ -5,6 +5,7 @@ import concourse.mybir as mybir
 F32 = mybir.dt.float32
 I32 = mybir.dt.int32
 U8 = mybir.dt.uint8
+BF16 = mybir.dt.bfloat16
 FP4X4 = mybir.dt.float4_e2m1fn_x4
 ALU = mybir.AluOpType
 ACT = mybir.ActivationFunctionType
@@ -63,6 +64,8 @@ def tile_stickyllamaattention_pa_kernel(tc, xw, xs, wqw, wqs, wkw, wks, out_0, o
         wc_r = [keep.tile([P, PASSES, 1024], U8, name="wc_r%d" % b, align_bytes=64) for b in range(4)]
         ws_r = [keep.tile([P, PASSES, 512], U8, name="ws_r%d" % b, align_bytes=64) for b in range(4)]
 
+        idle_in = keep.tile([P, 512], BF16, name="idle_in")
+
         def load_quadrant(plane, src, q):
             nc.sync.dma_start(
                 out=plane[32 * q : 32 * q + 32, 0, :].bitcast(I32),
@@ -88,6 +91,7 @@ def tile_stickyllamaattention_pa_kernel(tc, xw, xs, wqw, wqs, wkw, wks, out_0, o
                 load_codes(wc_0[g][:], wqw[g, :, 0:1024])
 
         pos_i = keep.tile([P, TOKEN_TILES], I32, name="pos_i")
+        nc.gpsimd.memset(idle_in[:], 0.0)
         nc.gpsimd.iota(out=pos_i[:], pattern=[[P, TOKEN_TILES]], base=0, channel_multiplier=1)
         for c in range(2):
             nc.gpsimd.memset(xs_b[c][:].bitcast(F32), 0.0)
@@ -197,6 +201,9 @@ def tile_stickyllamaattention_pa_kernel(tc, xw, xs, wqw, wqs, wkw, wks, out_0, o
 
         queues = (nc.scalar, nc.sync)
 
+        idle_out = psum.tile([P, 512], F32, name="acc")
+        for n in range(8):
+            nc.tensor.matmul(out=idle_out[:], lhsT=idle_in[:, 0:P], rhs=idle_in[:], start=True, stop=True)
         first = [psum.tile([P, 512], F32, name="acc") for i in range(8)]
         for g in range(PASSES):
             for i in range(8):

@@ -5,7 +5,6 @@ import concourse.mybir as mybir
 F32 = mybir.dt.float32
 I32 = mybir.dt.int32
 U8 = mybir.dt.uint8
-BF16 = mybir.dt.bfloat16
 FP4X4 = mybir.dt.float4_e2m1fn_x4
 ALU = mybir.AluOpType
 ACT = mybir.ActivationFunctionType
@@ -20,6 +19,7 @@ GRID = 2.0 ** -14
 FLOPS = 2 * 2048 * 4096 * 2560
 
 RUNS = ((0, 1), (1, 3), (3, 8))
+PAD_WC, PAD_WS, PAD_XC, PAD_XS = 0, 64, 128, 192
 
 
 def turns_per_position():
@@ -55,16 +55,18 @@ def tile_stickyllamaattention_pa_kernel(tc, xw, xs, wqw, wqs, wkw, wks, out_0, o
                     in_=src[:, 4 * q : 4 * q + 4, :].rearrange("g r n -> r g n").bitcast(I32),
                 )
 
-        xc_a = [keep.tile([P, 2048], U8, name="xc_a%d" % g, align_bytes=64) for g in range(PASSES)]
-        wc_0 = [keep.tile([P, 1024], U8, name="wc_0%d" % g, align_bytes=64) for g in range(PASSES)]
-        xs_a = [keep.tile([P, b - a, 1024], U8, name="xs_a%d" % a, align_bytes=64) for a, b in RUNS]
-        ws_0 = [keep.tile([P, b - a, 512], U8, name="ws_0%d" % a, align_bytes=64) for a, b in RUNS]
-        xc_b = [keep.tile([P, PASSES, 1024], U8, name="xc_b%d" % c, align_bytes=64) for c in range(2)]
-        xs_b = [keep.tile([P, PASSES, 512], U8, name="xs_b%d" % c, align_bytes=64) for c in range(2)]
-        wc_r = [keep.tile([P, PASSES, 1024], U8, name="wc_r%d" % b, align_bytes=64) for b in range(4)]
-        ws_r = [keep.tile([P, PASSES, 512], U8, name="ws_r%d" % b, align_bytes=64) for b in range(4)]
+        def operand(name, passes, width, pad):
+            whole = keep.tile([P, pad + passes * width], U8, name=name, align_bytes=256)
+            return whole[:, pad : pad + passes * width].rearrange("p (g n) -> p g n", g=passes)
 
-        idle_in = keep.tile([P, 512], BF16, name="idle_in")
+        xc_a = [operand("xc_a%d" % g, 1, 2048, PAD_XC) for g in range(PASSES)]
+        wc_0 = [operand("wc_0%d" % g, 1, 1024, PAD_WC) for g in range(PASSES)]
+        xs_a = [operand("xs_a%d" % a, b - a, 1024, PAD_XS) for a, b in RUNS]
+        ws_0 = [operand("ws_0%d" % a, b - a, 512, PAD_WS) for a, b in RUNS]
+        xc_b = [operand("xc_b%d" % c, PASSES, 1024, PAD_XC) for c in range(2)]
+        xs_b = [operand("xs_b%d" % c, PASSES, 512, PAD_XS) for c in range(2)]
+        wc_r = [operand("wc_r%d" % b, PASSES, 1024, PAD_WC) for b in range(4)]
+        ws_r = [operand("ws_r%d" % b, PASSES, 512, PAD_WS) for b in range(4)]
 
         def load_quadrant(plane, src, q):
             nc.sync.dma_start(
@@ -74,8 +76,8 @@ def tile_stickyllamaattention_pa_kernel(tc, xw, xs, wqw, wqs, wkw, wks, out_0, o
 
         load_quadrant(ws_0[0], wqs[:, :, 0:512], 0)
         load_quadrant(ws_0[0], wqs[:, :, 0:512], 1)
-        load_codes(xc_a[0][:], xw[0, :, 0:2048])
-        load_codes(wc_0[0][:], wqw[0, :, 0:1024])
+        load_codes(xc_a[0][:, 0, :], xw[0, :, 0:2048])
+        load_codes(wc_0[0][:, 0, :], wqw[0, :, 0:1024])
         load_quadrant(ws_0[0], wqs[:, :, 0:512], 2)
         load_quadrant(ws_0[0], wqs[:, :, 0:512], 3)
         for q in range(4):
@@ -87,11 +89,10 @@ def tile_stickyllamaattention_pa_kernel(tc, xw, xs, wqw, wqs, wkw, wks, out_0, o
             load_scales(xs_a[r], xs[a:b, :, 0:1024])
             load_scales(ws_0[r], wqs[a:b, :, 0:512])
             for g in range(a, b):
-                load_codes(xc_a[g][:], xw[g, :, 0:2048])
-                load_codes(wc_0[g][:], wqw[g, :, 0:1024])
+                load_codes(xc_a[g][:, 0, :], xw[g, :, 0:2048])
+                load_codes(wc_0[g][:, 0, :], wqw[g, :, 0:1024])
 
         pos_i = keep.tile([P, TOKEN_TILES], I32, name="pos_i")
-        nc.gpsimd.memset(idle_in[:], 0.0)
         nc.gpsimd.iota(out=pos_i[:], pattern=[[P, TOKEN_TILES]], base=0, channel_multiplier=1)
         for c in range(2):
             nc.gpsimd.memset(xs_b[c][:].bitcast(F32), 0.0)
@@ -156,14 +157,14 @@ def tile_stickyllamaattention_pa_kernel(tc, xw, xs, wqw, wqs, wkw, wks, out_0, o
         def x_ops(i, g):
             if i < 8:
                 r = run_of(g)
-                return (xc_a[g][:, 256 * i : 256 * (i + 1)], xs_a[r][:, g - RUNS[r][0], 128 * i : 128 * (i + 1)])
+                return (xc_a[g][:, 0, 256 * i : 256 * (i + 1)], xs_a[r][:, g - RUNS[r][0], 128 * i : 128 * (i + 1)])
             c, ii = divmod(i - 8, 4)
             return (xc_b[c][:, g, 256 * ii : 256 * (ii + 1)], xs_b[c][:, g, 128 * ii : 128 * (ii + 1)])
 
         def w_ops(b, g):
             if b == 0:
                 r = run_of(g)
-                return (wc_0[g][:, :], ws_0[r][:, g - RUNS[r][0], :])
+                return (wc_0[g][:, 0, :], ws_0[r][:, g - RUNS[r][0], :])
             return (wc_r[b - 1][:, g, :], ws_r[b - 1][:, g, :])
 
         def one_pass(acc, i, b, g, h0=0, nh=4):
@@ -201,9 +202,6 @@ def tile_stickyllamaattention_pa_kernel(tc, xw, xs, wqw, wqs, wkw, wks, out_0, o
 
         queues = (nc.scalar, nc.sync)
 
-        idle_out = psum.tile([P, 512], F32, name="acc")
-        for n in range(8):
-            nc.tensor.matmul(out=idle_out[:], lhsT=idle_in[:, 0:P], rhs=idle_in[:], start=True, stop=True)
         first = [psum.tile([P, 512], F32, name="acc") for i in range(8)]
         for g in range(PASSES):
             for i in range(8):

from contextlib import ExitStack

import concourse.mybir as mybir

F32 = mybir.dt.float32
I32 = mybir.dt.int32
U8 = mybir.dt.uint8
FP4X4 = mybir.dt.float4_e2m1fn_x4
ALU = mybir.AluOpType
ACT = mybir.ActivationFunctionType

P = 128
PASSES = 8
TOKEN_TILES = 16
HALF = 64
TWO_PI = 6.283185307179586
GRID = 2.0 ** -14

FLOPS = 2 * 2048 * 4096 * 2560

RUNS = ((0, 1), (1, 3), (3, 8))
PAD_WC, PAD_WS, PAD_XC, PAD_XS = 0, 64, 128, 192


def turns_per_position():
    g = []
    for j in range(HALF):
        inv = 1.0 / (500000.0 ** (2.0 * j / 128.0))
        wavelen = TWO_PI / inv
        smooth = min(max((8192.0 / wavelen - 1.0) / 3.0, 0.0), 1.0)
        g.append(((1.0 - smooth) * (inv / 8.0) + smooth * inv) / TWO_PI)
    return g


def tile_stickyllamaattention_pa_kernel(tc, xw, xs, wqw, wqs, wkw, wks, out_0, out_1):
    nc = tc.nc
    g_all = turns_per_position()
    g_hi = [int(g / GRID) * GRID for g in g_all]
    g_lo = [g - h for g, h in zip(g_all, g_hi)]
    n_hi = len([h for h in g_hi if h > 0.0])

    with ExitStack() as ctx:
        keep = ctx.enter_context(tc.tile_pool(name="keep", bufs=1))
        work = ctx.enter_context(tc.tile_pool(name="work", bufs=6))
        psum = ctx.enter_context(tc.psum_pool(name="acc", bufs=8))
        ctx.enter_context(tc.manual_schedule())

        def load_codes(tile_ap, src):
            nc.sync.dma_start(out=tile_ap.bitcast(I32), in_=src.bitcast(I32))

        def load_scales(plane, src):
            for q in range(4):
                nc.sync.dma_start(
                    out=plane[32 * q : 32 * q + 4, :, :].bitcast(I32),
                    in_=src[:, 4 * q : 4 * q + 4, :].rearrange("g r n -> r g n").bitcast(I32),
                )

        def operand(name, passes, width, pad):
            whole = keep.tile([P, pad + passes * width], U8, name=name, align_bytes=256)
            return whole[:, pad : pad + passes * width].rearrange("p (g n) -> p g n", g=passes)

        xc_a = [operand("xc_a%d" % g, 1, 2048, PAD_XC) for g in range(PASSES)]
        wc_0 = [operand("wc_0%d" % g, 1, 1024, PAD_WC) for g in range(PASSES)]
        xs_a = [operand("xs_a%d" % a, b - a, 1024, PAD_XS) for a, b in RUNS]
        ws_0 = [operand("ws_0%d" % a, b - a, 512, PAD_WS) for a, b in RUNS]
        xc_b = [operand("xc_b%d" % c, PASSES, 1024, PAD_XC) for c in range(2)]
        xs_b = [operand("xs_b%d" % c, PASSES, 512, PAD_XS) for c in range(2)]
        wc_r = [operand("wc_r%d" % b, PASSES, 1024, PAD_WC) for b in range(4)]
        ws_r = [operand("ws_r%d" % b, PASSES, 512, PAD_WS) for b in range(4)]

        def load_quadrant(plane, src, q):
            nc.sync.dma_start(
                out=plane[32 * q : 32 * q + 32, 0, :].bitcast(I32),
                in_=src.rearrange("g r n -> (g r) n")[4 * q : 4 * q + 32, :].bitcast(I32),
            )

        load_quadrant(ws_0[0], wqs[:, :, 0:512], 0)
        load_quadrant(ws_0[0], wqs[:, :, 0:512], 1)
        load_codes(xc_a[0][:, 0, :], xw[0, :, 0:2048])
        load_codes(wc_0[0][:, 0, :], wqw[0, :, 0:1024])
        load_quadrant(ws_0[0], wqs[:, :, 0:512], 2)
        load_quadrant(ws_0[0], wqs[:, :, 0:512], 3)
        for q in range(4):
            load_quadrant(xs_a[0], xs[:, :, 0:1024], q)
        for r in (1, 2):
            nc.vector.memset(xs_a[r][:].bitcast(I32), 0)
            nc.vector.memset(ws_0[r][:].bitcast(I32), 0)
        for r, (a, b) in ((1, RUNS[1]), (2, RUNS[2])):
            load_scales(xs_a[r], xs[a:b, :, 0:1024])
            load_scales(ws_0[r], wqs[a:b, :, 0:512])
            for g in range(a, b):
                load_codes(xc_a[g][:, 0, :], xw[g, :, 0:2048])
                load_codes(wc_0[g][:, 0, :], wqw[g, :, 0:1024])

        pos_i = keep.tile([P, TOKEN_TILES], I32, name="pos_i")
        nc.gpsimd.iota(out=pos_i[:], pattern=[[P, TOKEN_TILES]], base=0, channel_multiplier=1)
        for c in range(2):
            nc.gpsimd.memset(xs_b[c][:].bitcast(F32), 0.0)
        for b in range(4):
            nc.gpsimd.memset(ws_r[b][:].bitcast(F32), 0.0)

        for c in range(2):
            load_scales(xs_b[c], xs[:, :, 1024 + 512 * c : 1536 + 512 * c])
            load_codes(xc_b[c][:], xw[:, :, 2048 + 1024 * c : 3072 + 1024 * c].rearrange("g p n -> p g n"))
        for b in range(3):
            load_scales(ws_r[b], wqs[:, :, 512 * (b + 1) : 512 * (b + 2)])
            load_codes(wc_r[b][:], wqw[:, :, 1024 * (b + 1) : 1024 * (b + 2)].rearrange("g p n -> p g n"))
        load_scales(ws_r[3], wks[:, :, :])
        load_codes(wc_r[3][:], wkw[:, :, :].rearrange("g p n -> p g n"))

        warm = keep.tile([P, 1], F32, name="warm")
        nc.vector.memset(warm[:], 0.0)
        nc.scalar.activation(out=warm[:], in_=warm[:], func=ACT.Sin)

        pos_f = keep.tile([P, TOKEN_TILES], F32, name="pos_f")
        nc.vector.tensor_copy(out=pos_f[:], in_=pos_i[:])

        rr = keep.tile([P, TOKEN_TILES, HALF], F32, name="rr")
        big = keep.tile([P, TOKEN_TILES, n_hi], F32, name="big")
        whole_i = keep.tile([P, TOKEN_TILES, n_hi], I32, name="whole_i")
        whole_f = keep.tile([P, TOKEN_TILES, n_hi], F32, name="whole_f")
        neg_s = keep.tile([P, TOKEN_TILES, HALF], F32, name="neg_s")
        rc = keep.tile([P, TOKEN_TILES, HALF], F32, name="rc")
        neg_c = keep.tile([P, TOKEN_TILES, HALF], F32, name="neg_c")
        cos_t = keep.tile([P, TOKEN_TILES, HALF], F32, name="cos_t")
        sin_t = keep.tile([P, TOKEN_TILES, HALF], F32, name="sin_t")
        nsin_t = keep.tile([P, TOKEN_TILES, HALF], F32, name="nsin_t")

        for j in range(n_hi):
            nc.scalar.activation(out=big[:, :, j], in_=pos_f[:], func=ACT.Copy, scale=g_hi[j])
        for j in range(HALF):
            nc.vector.tensor_scalar(out=rr[:, :, j], in0=pos_f[:], scalar1=g_lo[j], scalar2=None, op0=ALU.mult)
        nc.vector.tensor_copy(out=whole_i[:], in_=big[:])
        nc.vector.tensor_copy(out=whole_f[:], in_=whole_i[:])
        nc.vector.tensor_tensor(out=big[:], in0=big[:], in1=whole_f[:], op=ALU.subtract)
        nc.vector.tensor_tensor(out=rr[:, :, 0:n_hi], in0=rr[:, :, 0:n_hi], in1=big[:], op=ALU.add)
        flat = "p i j -> p (i j)"
        nc.vector.scalar_tensor_tensor(
            out=neg_s[:].rearrange(flat), in0=rr[:].rearrange(flat), scalar=0.5, in1=rr[:].rearrange(flat),
            op0=ALU.is_gt, op1=ALU.subtract,
        )
        nc.vector.tensor_scalar(
            out=rc[:].rearrange(flat), in0=neg_s[:].rearrange(flat), scalar1=-1.0, scalar2=0.25,
            op0=ALU.mult, op1=ALU.add,
        )
        nc.scalar.activation(out=sin_t[:].rearrange(flat), in_=neg_s[:].rearrange(flat), func=ACT.Sin, scale=-TWO_PI)
        nc.scalar.activation(out=nsin_t[:].rearrange(flat), in_=neg_s[:].rearrange(flat), func=ACT.Sin, scale=TWO_PI)
        nc.vector.scalar_tensor_tensor(
            out=neg_c[:].rearrange(flat), in0=rc[:].rearrange(flat), scalar=0.5, in1=rc[:].rearrange(flat),
            op0=ALU.is_gt, op1=ALU.subtract,
        )
        nc.scalar.activation(out=cos_t[:].rearrange(flat), in_=neg_c[:].rearrange(flat), func=ACT.Sin, scale=-TWO_PI)

        def run_of(g):
            return [r for r, (a, b) in enumerate(RUNS) if a <= g < b][0]

        def x_ops(i, g):
            if i < 8:
                r = run_of(g)
                return (xc_a[g][:, 0, 256 * i : 256 * (i + 1)], xs_a[r][:, g - RUNS[r][0], 128 * i : 128 * (i + 1)])
            c, ii = divmod(i - 8, 4)
            return (xc_b[c][:, g, 256 * ii : 256 * (ii + 1)], xs_b[c][:, g, 128 * ii : 128 * (ii + 1)])

        def w_ops(b, g):
            if b == 0:
                r = run_of(g)
                return (wc_0[g][:, 0, :], ws_0[r][:, g - RUNS[r][0], :])
            return (wc_r[b - 1][:, g, :], ws_r[b - 1][:, g, :])

        def one_pass(acc, i, b, g, h0=0, nh=4):
            xcod, xsc = x_ops(i, g)
            wcod, wsc = w_ops(b, g)
            nc.tensor.matmul_mx(
                out=acc[:], lhsT=xcod.bitcast(FP4X4), lhsT_scale=xsc,
                rhs=wcod[:, 256 * h0 : 256 * (h0 + nh)].bitcast(FP4X4), rhs_scale=wsc[:, P * h0 : P * (h0 + nh)],
                start=(g == 0), stop=(g == PASSES - 1),
            )

        def rope_and_store(acc, i, b, adder, queue, h0=0, nh=4):
            res = work.tile([P, P * nh], F32, name="res", bufs=16)
            rot = work.tile([P, P * nh], F32, name="rot")
            nc.vector.tensor_tensor(
                out=res[:].rearrange("p (u j) -> p u j", j=HALF), in0=acc[:].rearrange("p (u j) -> p u j", j=HALF),
                in1=cos_t[:, i, :].unsqueeze(1).to_broadcast([P, 2 * nh, HALF]), op=ALU.mult,
            )
            a4 = acc[:].rearrange("p (h t j) -> p h t j", t=2, j=HALF)
            r4 = rot[:].rearrange("p (h t j) -> p h t j", t=2, j=HALF)
            nc.vector.tensor_tensor(
                out=r4[:, :, 0, :], in0=a4[:, :, 1, :],
                in1=nsin_t[:, i, :].unsqueeze(1).to_broadcast([P, nh, HALF]), op=ALU.mult,
            )
            nc.vector.tensor_tensor(
                out=r4[:, :, 1, :], in0=a4[:, :, 0, :],
                in1=sin_t[:, i, :].unsqueeze(1).to_broadcast([P, nh, HALF]), op=ALU.mult,
            )
            adder.tensor_tensor(out=res[:], in0=res[:], in1=rot[:], op=ALU.add)
            dst = out_0[0, 4 * b + h0 : 4 * b + h0 + nh, :, :] if b < 4 else out_1[0, h0 : h0 + nh, :, :]
            queue.dma_start(
                out=dst[:, P * i : P * (i + 1), :].rearrange("h p d -> p h d"),
                in_=res[:].rearrange("p (h d) -> p h d", h=nh),
            )

        queues = (nc.scalar, nc.sync)

        first = [psum.tile([P, 512], F32, name="acc") for i in range(8)]
        for g in range(PASSES):
            for i in range(8):
                one_pass(first[i], i, 0, g)
        for i in range(8):
            rope_and_store(first[i], i, 0, nc.gpsimd, queues[i % 2])

        for b, i in [(b, i) for b in range(5) for i in range(TOKEN_TILES)][8:-1]:
            acc = psum.tile([P, 512], F32, name="acc")
            for g in range(PASSES):
                one_pass(acc, i, b, g)
            rope_and_store(acc, i, b, nc.gpsimd, queues[i % 2])

        for n, (h0, nh) in enumerate(((0, 2), (2, 2))):
            acc = psum.tile([P, P * nh], F32, name="acc")
            for g in range(PASSES):
                one_pass(acc, TOKEN_TILES - 1, 4, g, h0, nh)
            rope_and_store(acc, TOKEN_TILES - 1, 4, nc.vector, queues[(n + 1) % 2], h0, nh)
